import numpy as np
import ml_dtypes


def mxq(x, axis, fmt="e4m3"):
    dtype, down = {"e4m3": (ml_dtypes.float8_e4m3fn, 7), "e5m2": (ml_dtypes.float8_e5m2, 14)}[fmt]
    v = np.moveaxis(np.asarray(x, np.float32).astype(ml_dtypes.bfloat16).astype(np.float64), axis, -1)
    blocks = v.reshape(v.shape[:-1] + (-1, 32))
    amax = np.abs(blocks).max(-1, keepdims=True)
    byte = np.maximum(np.where(amax > 0, np.frexp(amax)[1] - 1 + 127, 0) - down, 1)
    scale = np.exp2(byte - 127.0)
    codes = (blocks / scale).astype(np.float32).astype(dtype).astype(np.float64)
    return np.moveaxis((codes * scale).reshape(v.shape), -1, axis)


WIDE = False


def mx_kscale(k):
    if not WIDE:
        return np.ones(k)
    levels = np.array([10, -10, 5, -5, 0])
    if k % 512:
        return np.exp2(np.random.permutation(np.resize(levels, k // 32))).repeat(32)
    a = np.empty((k // 512, 16))
    for p in range(k // 512):
        a[p, :8] = np.random.permutation(np.resize(levels, 8))
        for g in range(8):
            far = levels[np.abs(levels - a[p, g]) >= 10]
            a[p, g + 8] = far[np.random.randint(len(far))]
    return np.exp2(a.ravel()).repeat(32)


BF16 = ml_dtypes.bfloat16


def bf(x):
    return np.asarray(x, np.float32).astype(BF16)


def f64(x):
    return np.asarray(x).astype(np.float64)


B, S, D, H, DN, DR, DV, RQ, RKV = 4, 1024, 512, 8, 64, 64, 128, 512, 512
THETA = 10000.0
EPS = 1e-6


def rmsnorm(v, w):
    return v * (1.0 / np.sqrt(np.mean(v * v, axis=-1, keepdims=True) + EPS)) * w


def rotate_half(v):
    v1 = v[..., ::2]
    v2 = v[..., 1::2]
    return np.stack((-v2, v1), axis=-1).reshape(v.shape)


def rope_cache():
    inv_freq = 1.0 / THETA ** (np.arange(0, DR, 2) / DR)
    freqs = np.outer(np.arange(S), inv_freq)
    emb = np.concatenate((freqs, freqs), -1)
    return np.cos(emb), np.sin(emb)


def apply_rope(v, cos, sin):
    return v * cos[None, None] + rotate_half(v) * sin[None, None]


def setup_inputs():
    s, t = mx_kscale(D), mx_kscale(RQ)
    return {"x": bf(np.random.standard_normal((B, S, D)) * s),
            "Wqa": bf(np.random.standard_normal((D, RQ)) / np.sqrt(D) / s[:, None]),
            "q_a_norm_w": bf((1.0 + 0.1 * np.random.standard_normal(RQ)) * t),
            "Wqb": bf(np.random.standard_normal((RQ, H * (DN + DR))) / np.sqrt(RQ) / t[:, None])}


def reference(x, Wqa, q_a_norm_w, Wqb):
    c = mxq(f64(x), 2, "e4m3") @ mxq(f64(Wqa), 0, "e4m3")
    h = rmsnorm(c, f64(q_a_norm_w))
    q = mxq(h, 2, "e4m3") @ mxq(f64(Wqb), 0, "e4m3")
    q = q.reshape(B, S, H, DN + DR).transpose(0, 2, 1, 3)
    q_nope, q_rope = q[..., :DN], q[..., DN:]
    cos, sin = rope_cache()
    q_rope = apply_rope(q_rope, cos, sin)
    return np.concatenate([q_nope, q_rope], -1)

@@ -1,0 +1,370 @@
+import math
+from contextlib import ExitStack
+
+import concourse.bass as bass
+import concourse.masks as masks
+import concourse.mybir as mybir
+import concourse.tile as tile
+
+F32 = mybir.dt.float32
+BF16 = mybir.dt.bfloat16
+I32 = mybir.dt.int32
+U32 = mybir.dt.uint32
+U8 = mybir.dt.uint8
+FP8X4 = mybir.dt.float8_e4m3fn_x4
+ALU = mybir.AluOpType
+ACT = mybir.ActivationFunctionType
+
+P = 128
+HEADS = 8
+N_UNITS = 8
+N_PAIRS = 16
+EPS = 1e-6
+FLOPS = 2 * 4096 * 512 * 512 + 2 * 4096 * 512 * 1024
+
+
+def tile_multiheadlatentattention_pa_t_kernel(tc, x, Wqa, q_a_norm_w, Wqb, out):
+    nc = tc.nc
+    with ExitStack() as ctx:
+        ctx.enter_context(tc.manual_schedule())
+        const = ctx.enter_context(tc.tile_pool(name="const", bufs=1))
+        psum = ctx.enter_context(tc.psum_pool(name="psum", bufs=1))
+        work = ctx.enter_context(tc.tile_pool(name="work", bufs=3))
+        outp = ctx.enter_context(tc.tile_pool(name="outp", bufs=3))
+
+        x_units = x.flatten_outer_dims().rearrange("(u p i) d -> u p (i d)", u=N_UNITS, p=P, i=4)
+        wa_raw = const.tile([P, 4, 512], BF16, name="wa_raw")
+        nc.sync.dma_start(
+            out=wa_raw[:].rearrange("p j c -> p (j c)"),
+            in_=Wqa.rearrange("(p j) c -> p (j c)", p=P, j=4),
+        )
+        x_sb = []
+        for u in range(N_UNITS):
+            x_sb.append(const.tile([P, 2048], BF16, name="x_sb%d" % u))
+        nc.sync.dma_start(out=x_sb[0][:, 0:1024], in_=x_units[0][:, 0:1024])
+        nc.sync.dma_start(out=x_sb[0][:, 1024:2048], in_=x_units[0][:, 1024:2048])
+        w_row = const.tile([P, 512], BF16, name="w_row")
+        nc.gpsimd.memset(w_row[:], 0.0)
+        nc.sync.dma_start(out=w_row[0:1, :], in_=q_a_norm_w.rearrange("(o r) -> o r", o=1))
+        for u in range(1, 4):
+            nc.sync.dma_start(out=x_sb[u][:], in_=x_units[u])
+        wb_raw = const.tile([P, 4, 1024], BF16, name="wb_raw")
+        nc.sync.dma_start(
+            out=wb_raw[:].rearrange("p j n -> p (j n)"), in_=Wqb.rearrange("(p j) n -> p (j n)", p=P, j=4)
+        )
+        for u in range(4, N_UNITS):
+            nc.sync.dma_start(out=x_sb[u][:], in_=x_units[u])
+
+        pos_i = const.tile([P, 8], I32, name="pos_i")
+        nc.gpsimd.iota(pos_i[:], pattern=[[512, 2], [1, 4]], base=0, channel_multiplier=4)
+        ident_f = const.tile([P, P], F32, name="ident_f")
+        masks.make_identity(nc, ident_f[:])
+        ident_b = const.tile([P, P], BF16, name="ident_b")
+        masks.make_identity(nc, ident_b[:])
+        eps_t = const.tile([P, 1], F32, name="eps_t")
+        nc.vector.memset(eps_t[:], EPS)
+        ones_b = const.tile([P, P], BF16, name="ones_b")
+        nc.gpsimd.memset(ones_b[:], 1.0)
+        w_bc = const.tile([P, 512], BF16, name="w_bc")
+
+        def spread_gain():
+            w_ps = psum.tile([P, 512], F32, name="w_ps", tag="ht")
+            nc.tensor.matmul(out=w_ps[:], lhsT=ones_b[:], rhs=w_row[:], start=True, stop=True)
+            nc.vector.tensor_copy(
+                out=w_bc[:].rearrange("p (t m) -> p t m", t=4), in_=w_ps[:].rearrange("p (m t) -> p t m", t=4)
+            )
+
+        ratio = 10000.0 ** (-1.0 / 32.0)
+        turn = const.tile([P, 32], F32, name="turn")
+        one = const.tile([P, 1], F32, name="one")
+        nc.vector.memset(one[:], 1.0)
+        nc.vector.tensor_scalar_mul(out=turn[:, 0:1], in0=one[:], scalar1=1.0 / (2.0 * math.pi))
+        nc.vector.tensor_scalar_mul(out=turn[:, 1:2], in0=one[:], scalar1=ratio / (2.0 * math.pi))
+        for n in (2, 4, 8, 16):
+            nc.vector.tensor_scalar_mul(out=turn[:, n : 2 * n], in0=turn[:, 0:n], scalar1=ratio**n)
+        pos_f = const.tile([P, 8], F32, name="pos_f")
+        nc.vector.tensor_copy(out=pos_f[:], in_=pos_i[:])
+        turns = const.tile([P, 2, 8, 32], F32, name="turns")
+        nc.vector.tensor_tensor(
+            out=turns[:, 0],
+            in0=pos_f[:].unsqueeze(2).to_broadcast([P, 8, 32]),
+            in1=turn[:].unsqueeze(1).to_broadcast([P, 8, 32]),
+            op=ALU.mult,
+        )
+        nc.vector.tensor_scalar_add(out=turns[:, 1], in0=turns[:, 0], scalar1=0.25)
+        turns_flat = turns[:].rearrange("p s c f -> p (s c f)")
+        whole_i = const.tile([P, 512], I32, name="whole_i")
+        nc.vector.tensor_copy(out=whole_i[:], in_=turns_flat)
+        whole_f = const.tile([P, 512], F32, name="whole_f")
+        nc.vector.tensor_copy(out=whole_f[:], in_=whole_i[:])
+        frac = const.tile([P, 512], F32, name="frac")
+        nc.vector.tensor_tensor(out=frac[:], in0=turns_flat, in1=whole_f[:], op=ALU.subtract)
+        sincos = const.tile([P, 2, 8, 32], F32, name="sincos")
+        warm = const.tile([P, 2], F32, name="warm")
+        nc.scalar.activation(out=warm[:, 0:1], in_=one[:], func=ACT.Sin)
+        tab = const.tile([P, 8, 2, 2, 32], F32, name="tab")
+
+        def tables():
+            nc.scalar.activation(
+                out=sincos[:].rearrange("p s c f -> p (s c f)"), in_=frac[:], func=ACT.Sin, scale=2.0 * math.pi
+            )
+            nc.scalar.activation(out=warm[:, 1:2], in_=eps_t[:], func=ACT.Abs_reciprocal_sqrt)
+            nc.gpsimd.tensor_scalar(
+                out=tab[:, :, 0],
+                in0=sincos[:, 1].unsqueeze(2).to_broadcast([P, 8, 2, 32]),
+                scalar1=1.0,
+                scalar2=0.0,
+                op0=ALU.mult,
+                op1=ALU.add,
+            )
+            for e in range(2):
+                nc.gpsimd.tensor_scalar(
+                    out=tab[:, :, 1].rearrange("p c s (j e) -> p c s j e", e=2)[:, :, :, :, e],
+                    in0=sincos[:, 0]
+                    .rearrange("p c (j e) -> p c j e", e=2)[:, :, :, 1 - e]
+                    .unsqueeze(2)
+                    .to_broadcast([P, 8, 2, 16]),
+                    scalar1=1.0 if e == 0 else -1.0,
+                    scalar2=0.0,
+                    op0=ALU.mult,
+                    op1=ALU.add,
+                )
+
+        wa_grp = const.tile([P, 512, 4], BF16, name="wa_grp", align_bytes=64)
+        nc.vector.tensor_copy(
+            out=wa_grp[:].rearrange("p (t m) j -> p t m j", t=4),
+            in_=wa_raw[:].rearrange("p j (m t) -> p t m j", t=4),
+        )
+        wa_q = const.tile([P, 512], U32, name="wa_q", align_bytes=64)
+        wa_s = const.tile([P, 512], U8, name="wa_s", align_bytes=64)
+        nc.vector.quantize_mx(
+            out=wa_q[:].bitcast(FP8X4), scales=wa_s[:], in_=wa_grp[:].rearrange("p c t -> p (c t)")
+        )
+
+        wb_grp = const.tile([P, 1024, 4], BF16, name="wb_grp", align_bytes=64)
+        wb_q = const.tile([P, 1024], U32, name="wb_q", align_bytes=64)
+        wb_s = const.tile([P, 1024], U8, name="wb_s", align_bytes=64)
+
+        def wb_rope():
+            nc.vector.tensor_copy(
+                out=wb_grp[:, 512:1024, :].rearrange("p (h f) t -> p h f t", h=HEADS),
+                in_=wb_raw[:].rearrange("p t (h z f) -> p z h f t", h=HEADS, z=2)[:, 1],
+            )
+            nc.vector.quantize_mx(
+                out=wb_q[:, 512:1024].bitcast(FP8X4),
+                scales=wb_s[:, 512:1024],
+                in_=wb_grp[:, 512:1024, :].rearrange("p c t -> p (c t)"),
+            )
+
+        def wb_nope():
+            nc.vector.tensor_copy(
+                out=wb_grp[:, 0:512, :].rearrange("p (h f) t -> p h f t", h=HEADS),
+                in_=wb_raw[:].rearrange("p t (h z f) -> p z h f t", h=HEADS, z=2)[:, 0],
+            )
+            nc.vector.quantize_mx(
+                out=wb_q[:, 0:512].bitcast(FP8X4),
+                scales=wb_s[:, 0:512],
+                in_=wb_grp[:, 0:512, :].rearrange("p c t -> p (c t)"),
+            )
+
+        x_q = const.tile([P, N_PAIRS * 256], U32, name="x_q", align_bytes=64)
+        x_s = const.tile([P, N_PAIRS * 256], U8, name="x_s", align_bytes=64)
+
+        st = {}
+
+        def tx(p):
+            xt = psum.tile([P, 2, 2, P], F32, name="xt", tag=("r0", "n0", "r1", "n1")[p % 4])
+            st["xt", p] = xt
+            for a in range(2):
+                k = 2 * p + a
+                words = x_sb[k // 4][:].bitcast(F32)
+                for u in range(2):
+                    lo = (k % 4) * 256
+                    nc.tensor.transpose(xt[:, a, u, :], words[:, lo + u : lo + 256 : 2], ident_f[:])
+
+        def cx(p):
+            gx = work.tile([P, 1024], BF16, name="gx", tag="gx", bufs=4, align_bytes=64)
+            st["gx", p] = gx
+            dst = gx[:].bitcast(F32).rearrange("p (a r u) -> p a r u", a=2, u=2)
+            src = st["xt", p][:].rearrange("p a u r -> p a r u")
+            nc.scalar.copy(out=dst, in_=src)
+
+        def qx(p):
+            cols = slice(p * 256, (p + 1) * 256)
+            nc.vector.quantize_mx(out=x_q[:, cols].bitcast(FP8X4), scales=x_s[:, cols], in_=st["gx", p][:])
+
+        def m1(p, a):
+            k = 2 * p + a
+            c = psum.tile([P, 512], F32, name="c", tag="c%d" % (k % 3))
+            st["c", p, a] = c
+            nc.tensor.matmul_mx(
+                out=c[:],
+                lhsT=x_q[:, k * P : (k + 1) * P].bitcast(FP8X4),
+                lhsT_scale=x_s[:, k * P : (k + 1) * P],
+                rhs=wa_q[:].bitcast(FP8X4),
+                rhs_scale=wa_s[:],
+                start=True,
+                stop=True,
+            )
+
+        def sq(p, a):
+            ssq = work.tile([P, 1], F32, name="ssq", tag="ssq%d" % a)
+            st["ssq", p, a] = ssq
+            junk = work.tile([P, 512], BF16, name="junk", tag="junk")
+            nc.scalar.activation(out=junk[:], in_=st["c", p, a][:], func=ACT.Square, accum_out=ssq[:])
+
+        def sr(p, a):
+            rstd = work.tile([P, 1], F32, name="rstd", tag="rstd%d" % a)
+            st["rstd", p, a] = rstd
+            nc.scalar.activation(
+                out=rstd[:],
+                in_=st["ssq", p, a][:],
+                func=ACT.Abs_reciprocal_sqrt,
+                scale=1.0 / 512.0,
+                bias=eps_t[:],
+            )
+
+        def hh(p, a):
+            h = work.tile([P, 512], BF16, name="h%d" % a, tag="h%d" % a)
+            st["h", p, a] = h
+            nc.vector.scalar_tensor_tensor(
+                out=h[:],
+                in0=st["c", p, a][:],
+                scalar=st["rstd", p, a][:],
+                in1=w_bc[:],
+                op0=ALU.mult,
+                op1=ALU.mult,
+            )
+
+        def th(p):
+            ht = psum.tile([P, 2, 4, P], BF16, name="ht", tag="ht")
+            st["ht", p] = ht
+            for a in range(2):
+                for t in range(4):
+                    nc.tensor.matmul(
+                        out=ht[:, a, t, :], lhsT=st["h", p, a][:, t * P : (t + 1) * P], rhs=ident_b[:], start=True, stop=True
+                    )
+
+        def ch(p):
+            gh = work.tile([P, 1024], BF16, name="gh", tag="gh", align_bytes=64)
+            st["gh", p] = gh
+            nc.scalar.copy(
+                out=gh[:].rearrange("p (a r t) -> p a r t", a=2, t=4),
+                in_=st["ht", p][:].rearrange("p a t r -> p a r t"),
+            )
+
+        def qh(p):
+            hq = work.tile([P, 256], U32, name="hq", tag="hq", align_bytes=64)
+            hs = work.tile([P, 256], U8, name="hs", tag="hs", align_bytes=64)
+            st["hq", p] = (hq, hs)
+            nc.vector.quantize_mx(out=hq[:].bitcast(FP8X4), scales=hs[:], in_=st["gh", p][:])
+
+        def m2(p, a, z):
+            kind = "nr"[z]
+            acc = psum.tile([P, 512], F32, name="%s%d" % (kind, a), tag="%s%d" % (kind, a))
+            st[kind, p, a] = acc
+            hq, hs = st["hq", p]
+            nc.tensor.matmul_mx(
+                out=acc[:],
+                lhsT=hq[:, a * P : (a + 1) * P].bitcast(FP8X4),
+                lhsT_scale=hs[:, a * P : (a + 1) * P],
+                rhs=wb_q[:, z * 512 : (z + 1) * 512].bitcast(FP8X4),
+                rhs_scale=wb_s[:, z * 512 : (z + 1) * 512],
+                start=True,
+                stop=True,
+            )
+
+        def out_tile(u):
+            if ("o", u) not in st:
+                st["o", u] = outp.tile([P, HEADS, 4, P], F32, name="o_sb", tag="o_sb")
+            return st["o", u]
+
+        def cn(p, a):
+            k = 2 * p + a
+            nc.scalar.copy(
+                out=out_tile(k // 4)[:, :, k % 4, 0:64],
+                in_=st["n", p, a][:].rearrange("p (h f) -> p h f", h=HEADS),
+            )
+
+        def tt(p, a):
+            k = 2 * p + a
+            c = ((k // 4) % 2) * 4 + k % 4
+            prod = work.tile([P, 2, HEADS, 64], F32, name="prod", tag="prod")
+            st["t", p, a] = prod
+            nc.vector.tensor_tensor(
+                out=prod[:],
+                in0=st["r", p, a][:].rearrange("p (h f) -> p h f", h=HEADS).unsqueeze(1).to_broadcast([P, 2, HEADS, 64]),
+                in1=tab[:, c].rearrange("p z s f -> p z (s f)").unsqueeze(2).to_broadcast([P, 2, HEADS, 64]),
+                op=ALU.mult,
+            )
+
+        def ad(p, a):
+            k = 2 * p + a
+            prod = st["t", p, a]
+            engine = nc.vector if p == N_PAIRS - 1 else nc.gpsimd
+            engine.tensor_tensor(
+                out=out_tile(k // 4)[:, :, k % 4, 64:128].rearrange("p h (i e) -> p h i e", e=2),
+                in0=prod[:, 0].rearrange("p h (i e) -> p h i e", e=2),
+                in1=prod[:, 1].rearrange("p h (i e) -> p h i e", e=2)[:, :, :, ::-1],
+                op=ALU.add,
+            )
+
+        def store(u, lo, hi):
+            dst = out[u // 2].rearrange("h (q p i) f -> q p h (i f)", q=2, p=P, i=4)[u % 2]
+            nc.sync.dma_start(
+                out=dst[:, :, lo * P : hi * P],
+                in_=st["o", u][:, :, lo:hi, :].rearrange("p h i f -> p h (i f)"),
+            )
+
+        def done(p, a):
+            if p == N_PAIRS - 1:
+                store(N_UNITS - 1, 2 + a, 3 + a)
+            elif p == N_PAIRS - 2 and a == 1:
+                store(N_UNITS - 1, 0, 2)
+            elif p % 2 == 1 and a == 1:
+                store(p // 2, 0, 4)
+
+        def run(stage, p, *rest):
+            if 0 <= p < N_PAIRS:
+                stage(p, *rest)
+
+        def x_stage(q):
+            run(tx, q)
+            run(cx, q - 2)
+            run(qx, q - 3)
+            if q == 3:
+                spread_gain()
+
+        tables()
+        for n in range(-1, N_PAIRS + 4):
+            x_stage(4 * n + 4)
+            run(m1, n, 0)
+            run(m2, n - 3, 0, 1)
+            run(hh, n - 1, 1)
+            run(m1, n, 1)
+            run(tt, n - 3, 0)
+            x_stage(4 * n + 5)
+            run(ch, n - 2)
+            run(sq, n, 0)
+            run(ad, n - 4, 0)
+            run(done, n - 4, 0)
+            run(sq, n, 1)
+            run(sr, n, 0)
+            x_stage(4 * n + 6)
+            run(m2, n - 3, 0, 0)
+            run(m2, n - 3, 1, 1)
+            run(cn, n - 3, 0)
+            run(m2, n - 3, 1, 0)
+            run(qh, n - 2)
+            run(th, n - 1)
+            run(sr, n, 1)
+            x_stage(4 * n + 7)
+            run(cn, n - 3, 1)
+            run(hh, n, 0)
+            run(ad, n - 4, 1)
+            run(done, n - 4, 1)
+            run(tt, n - 3, 1)
+            if n == 0:
+                wb_rope()
+            if n == 1:
+                wb_nope()

@@ -274,15 +274,24 @@ def tile_multiheadlatentattention_pa_t_kernel(tc, x, Wqa, q_a_norm_w, Wqb, out):
                 stop=True,
             )
 
-        def out_tile(u):
-            if ("o", u) not in st:
-                st["o", u] = outp.tile([P, HEADS, 4, P], F32, name="o_sb", tag="o_sb")
-            return st["o", u]
+        def out_part(k):
+            u, i = divmod(k, 4)
+            if u < N_UNITS - 2:
+                first, width = 0, 4
+            elif u == N_UNITS - 2 or i < 2:
+                first, width = i // 2 * 2, 2
+            else:
+                first, width = i, 1
+            if ("o", u, first) not in st:
+                st["o", u, first] = outp.tile(
+                    [P, HEADS, width, P], F32, name="o_sb", tag="o_sb%d" % width, bufs=2 if width == 1 else 3
+                )
+            return st["o", u, first][:, :, i - first, :]
 
         def cn(p, a):
             k = 2 * p + a
             nc.scalar.copy(
-                out=out_tile(k // 4)[:, :, k % 4, 0:64],
+                out=out_part(k)[:, :, 0:64],
                 in_=st["n", p, a][:].rearrange("p (h f) -> p h f", h=HEADS),
             )
 
@@ -303,7 +312,7 @@ def tile_multiheadlatentattention_pa_t_kernel(tc, x, Wqa, q_a_norm_w, Wqb, out):
             prod = st["t", p, a]
             engine = nc.vector if p == N_PAIRS - 1 else nc.gpsimd
             engine.tensor_tensor(
-                out=out_tile(k // 4)[:, :, k % 4, 64:128].rearrange("p h (i e) -> p h i e", e=2),
+                out=out_part(k)[:, :, 64:128].rearrange("p h (i e) -> p h i e", e=2),
                 in0=prod[:, 0].rearrange("p h (i e) -> p h i e", e=2),
                 in1=prod[:, 1].rearrange("p h (i e) -> p h i e", e=2)[:, :, :, ::-1],
                 op=ALU.add,
@@ -313,14 +322,14 @@ def tile_multiheadlatentattention_pa_t_kernel(tc, x, Wqa, q_a_norm_w, Wqb, out):
             dst = out[u // 2].rearrange("h (q p i) f -> q p h (i f)", q=2, p=P, i=4)[u % 2]
             nc.sync.dma_start(
                 out=dst[:, :, lo * P : hi * P],
-                in_=st["o", u][:, :, lo:hi, :].rearrange("p h i f -> p h (i f)"),
+                in_=st["o", u, lo][:].rearrange("p h i f -> p h (i f)"),
             )
 
         def done(p, a):
             if p == N_PAIRS - 1:
                 store(N_UNITS - 1, 2 + a, 3 + a)
-            elif p == N_PAIRS - 2 and a == 1:
-                store(N_UNITS - 1, 0, 2)
+            elif p >= N_PAIRS - 4 and a == 1:
+                store(p // 2, p % 2 * 2, p % 2 * 2 + 2)
             elif p % 2 == 1 and a == 1:
                 store(p // 2, 0, 4)
 

@@ -59,8 +59,6 @@ def tile_multiheadlatentattention_pa_t_kernel(tc, x, Wqa, q_a_norm_w, Wqb, out):
         nc.gpsimd.iota(pos_i[:], pattern=[[512, 2], [1, 4]], base=0, channel_multiplier=4)
         ident_f = const.tile([P, P], F32, name="ident_f")
         masks.make_identity(nc, ident_f[:])
-        ident_b = const.tile([P, P], BF16, name="ident_b")
-        masks.make_identity(nc, ident_b[:])
         eps_t = const.tile([P, 1], F32, name="eps_t")
         nc.vector.memset(eps_t[:], EPS)
         ones_b = const.tile([P, P], BF16, name="ones_b")
@@ -71,7 +69,8 @@ def tile_multiheadlatentattention_pa_t_kernel(tc, x, Wqa, q_a_norm_w, Wqb, out):
             w_ps = psum.tile([P, 512], F32, name="w_ps", tag="ht")
             nc.tensor.matmul(out=w_ps[:], lhsT=ones_b[:], rhs=w_row[:], start=True, stop=True)
             nc.vector.tensor_copy(
-                out=w_bc[:].rearrange("p (t m) -> p t m", t=4), in_=w_ps[:].rearrange("p (m t) -> p t m", t=4)
+                out=w_bc[:].rearrange("p (u m e) -> p u m e", u=2, e=2),
+                in_=w_ps[:].rearrange("p (m u e) -> p u m e", u=2, e=2),
             )
 
         ratio = 10000.0 ** (-1.0 / 32.0)
@@ -131,10 +130,11 @@ def tile_multiheadlatentattention_pa_t_kernel(tc, x, Wqa, q_a_norm_w, Wqb, out):
                 )
 
         wa_grp = const.tile([P, 512, 4], BF16, name="wa_grp", align_bytes=64)
-        nc.vector.tensor_copy(
-            out=wa_grp[:].rearrange("p (t m) j -> p t m j", t=4),
-            in_=wa_raw[:].rearrange("p j (m t) -> p t m j", t=4),
-        )
+        for u in range(2):
+            nc.vector.tensor_copy(
+                out=wa_grp[:].rearrange("p (u m e) j -> p u m e j", u=2, e=2)[:, u],
+                in_=wa_raw[:].rearrange("p j (m u e) -> p u m e j", u=2, e=2)[:, u],
+            )
         wa_q = const.tile([P, 512], U32, name="wa_q", align_bytes=64)
         wa_s = const.tile([P, 512], U8, name="wa_s", align_bytes=64)
         nc.vector.quantize_mx(
@@ -237,20 +237,19 @@ def tile_multiheadlatentattention_pa_t_kernel(tc, x, Wqa, q_a_norm_w, Wqb, out):
             )
 
         def th(p):
-            ht = psum.tile([P, 2, 4, P], BF16, name="ht", tag="ht")
+            ht = psum.tile([P, 2, 2, P], F32, name="ht", tag="ht")
             st["ht", p] = ht
             for a in range(2):
-                for t in range(4):
-                    nc.tensor.matmul(
-                        out=ht[:, a, t, :], lhsT=st["h", p, a][:, t * P : (t + 1) * P], rhs=ident_b[:], start=True, stop=True
-                    )
+                words = st["h", p, a][:].bitcast(F32)
+                for u in range(2):
+                    nc.tensor.transpose(ht[:, a, u, :], words[:, u * P : (u + 1) * P], ident_f[:])
 
         def ch(p):
             gh = work.tile([P, 1024], BF16, name="gh", tag="gh", align_bytes=64)
             st["gh", p] = gh
             nc.scalar.copy(
-                out=gh[:].rearrange("p (a r t) -> p a r t", a=2, t=4),
-                in_=st["ht", p][:].rearrange("p a t r -> p a r t"),
+                out=gh[:].bitcast(F32).rearrange("p (a r u) -> p a r u", a=2, u=2),
+                in_=st["ht", p][:].rearrange("p a u r -> p a r u"),
             )
 
         def qh(p):

@@ -20,6 +20,7 @@ HEADS = 8
 N_UNITS = 8
 N_PAIRS = 16
 EPS = 1e-6
+SHARE = (0, 2)
 FLOPS = 2 * 4096 * 512 * 512 + 2 * 4096 * 512 * 1024
 
 
@@ -33,6 +34,9 @@ def tile_multiheadlatentattention_pa_t_kernel(tc, x, Wqa, q_a_norm_w, Wqb, out):
         outp = ctx.enter_context(tc.tile_pool(name="outp", bufs=3))
 
         x_units = x.flatten_outer_dims().rearrange("(u p i) d -> u p (i d)", u=N_UNITS, p=P, i=4)
+        w_row = const.tile([P, 512], BF16, name="w_row")
+        nc.gpsimd.memset(w_row[:], 0.0)
+        nc.sync.dma_start(out=w_row[0:1, :], in_=q_a_norm_w.rearrange("(o r) -> o r", o=1))
         wa_raw = const.tile([P, 4, 512], BF16, name="wa_raw")
         nc.sync.dma_start(
             out=wa_raw[:].rearrange("p j c -> p (j c)"),
@@ -43,20 +47,17 @@ def tile_multiheadlatentattention_pa_t_kernel(tc, x, Wqa, q_a_norm_w, Wqb, out):
             x_sb.append(const.tile([P, 2048], BF16, name="x_sb%d" % u))
         nc.sync.dma_start(out=x_sb[0][:, 0:1024], in_=x_units[0][:, 0:1024])
         nc.sync.dma_start(out=x_sb[0][:, 1024:2048], in_=x_units[0][:, 1024:2048])
-        w_row = const.tile([P, 512], BF16, name="w_row")
-        nc.gpsimd.memset(w_row[:], 0.0)
-        nc.sync.dma_start(out=w_row[0:1, :], in_=q_a_norm_w.rearrange("(o r) -> o r", o=1))
-        for u in range(1, 4):
+        for u in range(1, 6):
             nc.sync.dma_start(out=x_sb[u][:], in_=x_units[u])
         wb_raw = const.tile([P, 4, 1024], BF16, name="wb_raw")
         nc.sync.dma_start(
             out=wb_raw[:].rearrange("p j n -> p (j n)"), in_=Wqb.rearrange("(p j) n -> p (j n)", p=P, j=4)
         )
-        for u in range(4, N_UNITS):
+        for u in range(6, N_UNITS):
             nc.sync.dma_start(out=x_sb[u][:], in_=x_units[u])
 
-        pos_i = const.tile([P, 8], I32, name="pos_i")
-        nc.gpsimd.iota(pos_i[:], pattern=[[512, 2], [1, 4]], base=0, channel_multiplier=4)
+        pos = const.tile([P, 8], I32, name="pos")
+        nc.gpsimd.iota(pos[:], pattern=[[512, 2], [1, 4]], base=0, channel_multiplier=4)
         ident_f = const.tile([P, P], F32, name="ident_f")
         masks.make_identity(nc, ident_f[:])
         eps_t = const.tile([P, 1], F32, name="eps_t")
@@ -74,55 +75,40 @@ def tile_multiheadlatentattention_pa_t_kernel(tc, x, Wqa, q_a_norm_w, Wqb, out):
             )
 
         ratio = 10000.0 ** (-1.0 / 32.0)
-        turn = const.tile([P, 32], F32, name="turn")
         one = const.tile([P, 1], F32, name="one")
         nc.vector.memset(one[:], 1.0)
-        nc.vector.tensor_scalar_mul(out=turn[:, 0:1], in0=one[:], scalar1=1.0 / (2.0 * math.pi))
-        nc.vector.tensor_scalar_mul(out=turn[:, 1:2], in0=one[:], scalar1=ratio / (2.0 * math.pi))
-        for n in (2, 4, 8, 16):
-            nc.vector.tensor_scalar_mul(out=turn[:, n : 2 * n], in0=turn[:, 0:n], scalar1=ratio**n)
-        pos_f = const.tile([P, 8], F32, name="pos_f")
-        nc.vector.tensor_copy(out=pos_f[:], in_=pos_i[:])
+        turn = const.tile([P, 32], F32, name="turn")
+        for f in range(4):
+            nc.vector.tensor_scalar_mul(out=turn[:, f : f + 1], in0=one[:], scalar1=ratio**f / (2.0 * math.pi))
+        for f in range(4, 32, 4):
+            nc.vector.tensor_scalar_mul(out=turn[:, f : f + 4], in0=turn[:, 0:4], scalar1=ratio**f)
         turns = const.tile([P, 2, 8, 32], F32, name="turns")
+        whole = const.tile([P, 2, 8, 32], I32, name="whole")
+        frac = const.tile([P, 2, 8, 32], F32, name="frac")
         nc.vector.tensor_tensor(
             out=turns[:, 0],
-            in0=pos_f[:].unsqueeze(2).to_broadcast([P, 8, 32]),
+            in0=pos[:].unsqueeze(2).to_broadcast([P, 8, 32]),
             in1=turn[:].unsqueeze(1).to_broadcast([P, 8, 32]),
             op=ALU.mult,
         )
         nc.vector.tensor_scalar_add(out=turns[:, 1], in0=turns[:, 0], scalar1=0.25)
-        turns_flat = turns[:].rearrange("p s c f -> p (s c f)")
-        whole_i = const.tile([P, 512], I32, name="whole_i")
-        nc.vector.tensor_copy(out=whole_i[:], in_=turns_flat)
-        whole_f = const.tile([P, 512], F32, name="whole_f")
-        nc.vector.tensor_copy(out=whole_f[:], in_=whole_i[:])
-        frac = const.tile([P, 512], F32, name="frac")
-        nc.vector.tensor_tensor(out=frac[:], in0=turns_flat, in1=whole_f[:], op=ALU.subtract)
-        sincos = const.tile([P, 2, 8, 32], F32, name="sincos")
+        for s in range(2):
+            nc.vector.tensor_copy(out=whole[:, s], in_=turns[:, s])
+        for s in range(2):
+            nc.vector.tensor_tensor(out=frac[:, s], in0=turns[:, s], in1=whole[:, s], op=ALU.subtract)
+        sines = const.tile([P, 8, 32], F32, name="sines")
         warm = const.tile([P, 2], F32, name="warm")
         nc.scalar.activation(out=warm[:, 0:1], in_=one[:], func=ACT.Sin)
-        tab = const.tile([P, 8, 2, 2, 32], F32, name="tab")
+        tab = const.tile([P, 8, 2, 32], F32, name="tab")
 
         def tables():
-            nc.scalar.activation(
-                out=sincos[:].rearrange("p s c f -> p (s c f)"), in_=frac[:], func=ACT.Sin, scale=2.0 * math.pi
-            )
+            nc.scalar.activation(out=sines[:], in_=frac[:, 0], func=ACT.Sin, scale=2.0 * math.pi)
+            nc.scalar.activation(out=tab[:, :, 0], in_=frac[:, 1], func=ACT.Sin, scale=2.0 * math.pi)
             nc.scalar.activation(out=warm[:, 1:2], in_=eps_t[:], func=ACT.Abs_reciprocal_sqrt)
-            nc.gpsimd.tensor_scalar(
-                out=tab[:, :, 0],
-                in0=sincos[:, 1].unsqueeze(2).to_broadcast([P, 8, 2, 32]),
-                scalar1=1.0,
-                scalar2=0.0,
-                op0=ALU.mult,
-                op1=ALU.add,
-            )
             for e in range(2):
                 nc.gpsimd.tensor_scalar(
-                    out=tab[:, :, 1].rearrange("p c s (j e) -> p c s j e", e=2)[:, :, :, :, e],
-                    in0=sincos[:, 0]
-                    .rearrange("p c (j e) -> p c j e", e=2)[:, :, :, 1 - e]
-                    .unsqueeze(2)
-                    .to_broadcast([P, 8, 2, 16]),
+                    out=tab[:, :, 1].rearrange("p c (j e) -> p c j e", e=2)[:, :, :, e],
+                    in0=sines[:].rearrange("p c (j e) -> p c j e", e=2)[:, :, :, 1 - e],
                     scalar1=1.0 if e == 0 else -1.0,
                     scalar2=0.0,
                     op0=ALU.mult,
@@ -208,17 +194,17 @@ def tile_multiheadlatentattention_pa_t_kernel(tc, x, Wqa, q_a_norm_w, Wqb, out):
             )
 
         def sq(p, a):
-            ssq = work.tile([P, 1], F32, name="ssq", tag="ssq%d" % a)
-            st["ssq", p, a] = ssq
+            if a == 0:
+                st["ssq", p] = work.tile([P, 2], F32, name="ssq", tag="ssq")
             junk = work.tile([P, 512], BF16, name="junk", tag="junk")
-            nc.scalar.activation(out=junk[:], in_=st["c", p, a][:], func=ACT.Square, accum_out=ssq[:])
+            nc.scalar.activation(out=junk[:], in_=st["c", p, a][:], func=ACT.Square, accum_out=st["ssq", p][:, a : a + 1])
 
-        def sr(p, a):
-            rstd = work.tile([P, 1], F32, name="rstd", tag="rstd%d" % a)
-            st["rstd", p, a] = rstd
+        def sr(p):
+            rstd = work.tile([P, 2], F32, name="rstd", tag="rstd")
+            st["rstd", p] = rstd
             nc.scalar.activation(
                 out=rstd[:],
-                in_=st["ssq", p, a][:],
+                in_=st["ssq", p][:],
                 func=ACT.Abs_reciprocal_sqrt,
                 scale=1.0 / 512.0,
                 bias=eps_t[:],
@@ -230,7 +216,7 @@ def tile_multiheadlatentattention_pa_t_kernel(tc, x, Wqa, q_a_norm_w, Wqb, out):
             nc.vector.scalar_tensor_tensor(
                 out=h[:],
                 in0=st["c", p, a][:],
-                scalar=st["rstd", p, a][:],
+                scalar=st["rstd", p][:, a : a + 1],
                 in1=w_bc[:],
                 op0=ALU.mult,
                 op1=ALU.mult,
@@ -275,9 +261,9 @@ def tile_multiheadlatentattention_pa_t_kernel(tc, x, Wqa, q_a_norm_w, Wqb, out):
 
         def out_part(k):
             u, i = divmod(k, 4)
-            if u < N_UNITS - 2:
+            if u < N_UNITS - 3:
                 first, width = 0, 4
-            elif u == N_UNITS - 2 or i < 2:
+            elif u < N_UNITS - 1 or i < 2:
                 first, width = i // 2 * 2, 2
             else:
                 first, width = i, 1
@@ -294,17 +280,38 @@ def tile_multiheadlatentattention_pa_t_kernel(tc, x, Wqa, q_a_norm_w, Wqb, out):
                 in_=st["n", p, a][:].rearrange("p (h f) -> p h f", h=HEADS),
             )
 
-        def tt(p, a):
-            k = 2 * p + a
-            c = ((k // 4) % 2) * 4 + k % 4
-            prod = work.tile([P, 2, HEADS, 64], F32, name="prod", tag="prod")
-            st["t", p, a] = prod
-            nc.vector.tensor_tensor(
-                out=prod[:],
-                in0=st["r", p, a][:].rearrange("p (h f) -> p h f", h=HEADS).unsqueeze(1).to_broadcast([P, 2, HEADS, 64]),
-                in1=tab[:, c].rearrange("p z s f -> p z (s f)").unsqueeze(2).to_broadcast([P, 2, HEADS, 64]),
+        def prod_tile(p, a):
+            if ("t", p, a) not in st:
+                st["t", p, a] = work.tile([P, 2, 512], F32, name="prod", tag="prod")
+            return st["t", p, a]
+
+        def products(engine, p, a, r, lo, hi):
+            shape = [P, 2, 2 * (hi - lo), 32]
+            engine.tensor_tensor(
+                out=prod_tile(p, a)[:, :, lo * 64 : hi * 64].rearrange("p z (g f) -> p z g f", f=32),
+                in0=r.rearrange("p (g f) -> p g f", f=32).unsqueeze(1).to_broadcast(shape),
+                in1=tab[:, (2 * p + a) % 8].unsqueeze(2).to_broadcast(shape),
                 op=ALU.mult,
             )
+
+        def shared(p, a):
+            return SHARE[a] if p < N_PAIRS - 3 else 0
+
+        def tt(p, a):
+            hi = HEADS - shared(p, a)
+            products(nc.vector, p, a, st["r", p, a][:, 0 : hi * 64], 0, hi)
+
+        def cr(p, a):
+            s = shared(p, a)
+            if s:
+                r_sb = work.tile([P, s * 64], F32, name="r_sb", tag="r_sb%d" % a)
+                st["r_sb", p, a] = r_sb
+                nc.scalar.copy(out=r_sb[:], in_=st["r", p, a][:, 512 - s * 64 : 512])
+
+        def pr(p, a):
+            s = shared(p, a)
+            if s:
+                products(nc.gpsimd, p, a, st["r_sb", p, a][:], HEADS - s, HEADS)
 
         def ad(p, a):
             k = 2 * p + a
@@ -312,8 +319,8 @@ def tile_multiheadlatentattention_pa_t_kernel(tc, x, Wqa, q_a_norm_w, Wqb, out):
             engine = nc.vector if p == N_PAIRS - 1 else nc.gpsimd
             engine.tensor_tensor(
                 out=out_part(k)[:, :, 64:128].rearrange("p h (i e) -> p h i e", e=2),
-                in0=prod[:, 0].rearrange("p h (i e) -> p h i e", e=2),
-                in1=prod[:, 1].rearrange("p h (i e) -> p h i e", e=2)[:, :, :, ::-1],
+                in0=prod[:, 0].rearrange("p (h i e) -> p h i e", h=HEADS, e=2),
+                in1=prod[:, 1].rearrange("p (h i e) -> p h i e", h=HEADS, e=2)[:, :, :, ::-1],
                 op=ALU.add,
             )
 
@@ -327,7 +334,7 @@ def tile_multiheadlatentattention_pa_t_kernel(tc, x, Wqa, q_a_norm_w, Wqb, out):
         def done(p, a):
             if p == N_PAIRS - 1:
                 store(N_UNITS - 1, 2 + a, 3 + a)
-            elif p >= N_PAIRS - 4 and a == 1:
+            elif p >= N_PAIRS - 6 and a == 1:
                 store(p // 2, p % 2 * 2, p % 2 * 2 + 2)
             elif p % 2 == 1 and a == 1:
                 store(p // 2, 0, 4)
@@ -340,38 +347,38 @@ def tile_multiheadlatentattention_pa_t_kernel(tc, x, Wqa, q_a_norm_w, Wqb, out):
             run(tx, q)
             run(cx, q - 2)
             run(qx, q - 3)
-            if q == 3:
-                spread_gain()
 
         tables()
-        for n in range(-1, N_PAIRS + 4):
-            x_stage(4 * n + 4)
-            run(m1, n, 0)
-            run(m2, n - 3, 0, 1)
-            run(hh, n - 1, 1)
-            run(m1, n, 1)
+        spread_gain()
+        for n in range(-2, N_PAIRS + 4):
+            x_stage(4 * n + 8)
             run(tt, n - 3, 0)
-            x_stage(4 * n + 5)
-            run(ch, n - 2)
-            run(sq, n, 0)
-            run(ad, n - 4, 0)
-            run(done, n - 4, 0)
-            run(sq, n, 1)
-            run(sr, n, 0)
-            x_stage(4 * n + 6)
-            run(m2, n - 3, 0, 0)
-            run(m2, n - 3, 1, 1)
-            run(cn, n - 3, 0)
-            run(m2, n - 3, 1, 0)
-            run(qh, n - 2)
             run(th, n - 1)
-            run(sr, n, 1)
-            x_stage(4 * n + 7)
+            run(sq, n, 1)
+            run(ch, n - 1)
+            run(sr, n)
+            run(m1, n + 1, 0)
+            run(cn, n - 3, 0)
+            x_stage(4 * n + 9)
+            run(pr, n - 3, 1)
+            run(qh, n - 2)
+            run(ad, n - 3, 0)
+            run(done, n - 3, 0)
+            run(m2, n - 2, 0, 1)
+            run(m2, n - 2, 0, 0)
             run(cn, n - 3, 1)
-            run(hh, n, 0)
-            run(ad, n - 4, 1)
-            run(done, n - 4, 1)
             run(tt, n - 3, 1)
+            run(ad, n - 3, 1)
+            run(done, n - 3, 1)
+            x_stage(4 * n + 10)
+            run(sq, n + 1, 0)
+            run(m2, n - 2, 1, 1)
+            run(m2, n - 2, 1, 0)
+            run(cr, n - 2, 1)
+            run(hh, n, 0)
+            x_stage(4 * n + 11)
+            run(hh, n, 1)
+            run(m1, n + 1, 1)
             if n == 0:
                 wb_rope()
             if n == 1:

@@ -20,7 +20,7 @@ HEADS = 8
 N_UNITS = 8
 N_PAIRS = 16
 EPS = 1e-6
-SHARE = (0, 2)
+SHARE = (0, 1)
 FLOPS = 2 * 4096 * 512 * 512 + 2 * 4096 * 512 * 1024
 
 
@@ -351,15 +351,15 @@ def tile_multiheadlatentattention_pa_t_kernel(tc, x, Wqa, q_a_norm_w, Wqb, out):
         tables()
         spread_gain()
         for n in range(-2, N_PAIRS + 4):
-            x_stage(4 * n + 8)
+            x_stage(4 * n + 7)
             run(tt, n - 3, 0)
             run(th, n - 1)
             run(sq, n, 1)
             run(ch, n - 1)
             run(sr, n)
             run(m1, n + 1, 0)
+            x_stage(4 * n + 8)
             run(cn, n - 3, 0)
-            x_stage(4 * n + 9)
             run(pr, n - 3, 1)
             run(qh, n - 2)
             run(ad, n - 3, 0)
@@ -370,13 +370,13 @@ def tile_multiheadlatentattention_pa_t_kernel(tc, x, Wqa, q_a_norm_w, Wqb, out):
             run(tt, n - 3, 1)
             run(ad, n - 3, 1)
             run(done, n - 3, 1)
-            x_stage(4 * n + 10)
+            x_stage(4 * n + 9)
             run(sq, n + 1, 0)
             run(m2, n - 2, 1, 1)
             run(m2, n - 2, 1, 0)
             run(cr, n - 2, 1)
             run(hh, n, 0)
-            x_stage(4 * n + 11)
+            x_stage(4 * n + 10)
             run(hh, n, 1)
             run(m1, n + 1, 1)
             if n == 0:

@@ -168,16 +168,25 @@ def tile_multiheadlatentattention_pa_t_kernel(tc, x, Wqa, q_a_norm_w, Wqb, out):
                     lo = (k % 4) * 256
                     nc.tensor.transpose(xt[:, a, u, :], words[:, lo + u : lo + 256 : 2], ident_f[:])
 
+        def x_group(p):
+            return (p, 1) if p < 2 else (p // 2 * 2, 2)
+
         def cx(p):
-            gx = work.tile([P, 1024], BF16, name="gx", tag="gx", bufs=4, align_bytes=64)
-            st["gx", p] = gx
-            dst = gx[:].bitcast(F32).rearrange("p (a r u) -> p a r u", a=2, u=2)
+            first, pairs = x_group(p)
+            if p == first:
+                st["gx", first] = work.tile(
+                    [P, 1024 * pairs], BF16, name="gx", tag="gx%d" % pairs, bufs=4, align_bytes=64
+                )
+            at = (p - first) * 1024
+            dst = st["gx", first][:, at : at + 1024].bitcast(F32).rearrange("p (a r u) -> p a r u", a=2, u=2)
             src = st["xt", p][:].rearrange("p a u r -> p a r u")
             nc.scalar.copy(out=dst, in_=src)
 
         def qx(p):
-            cols = slice(p * 256, (p + 1) * 256)
-            nc.vector.quantize_mx(out=x_q[:, cols].bitcast(FP8X4), scales=x_s[:, cols], in_=st["gx", p][:])
+            first, pairs = x_group(p)
+            if p == first + pairs - 1:
+                cols = slice(first * 256, (p + 1) * 256)
+                nc.vector.quantize_mx(out=x_q[:, cols].bitcast(FP8X4), scales=x_s[:, cols], in_=st["gx", first][:])
 
         def m1(p, a):
             k = 2 * p + a
@@ -351,13 +360,17 @@ def tile_multiheadlatentattention_pa_t_kernel(tc, x, Wqa, q_a_norm_w, Wqb, out):
         tables()
         spread_gain()
         for n in range(-2, N_PAIRS + 4):
-            x_stage(4 * n + 7)
             run(tt, n - 3, 0)
             run(th, n - 1)
-            run(sq, n, 1)
+            x_stage(4 * n + 7)
+            if n > 0:
+                run(sq, n, 1)
             run(ch, n - 1)
-            run(sr, n)
+            if n > 0:
+                run(sr, n)
             run(m1, n + 1, 0)
+            if n == -1:
+                m1(0, 1)
             x_stage(4 * n + 8)
             run(cn, n - 3, 0)
             run(pr, n - 3, 1)
@@ -372,13 +385,17 @@ def tile_multiheadlatentattention_pa_t_kernel(tc, x, Wqa, q_a_norm_w, Wqb, out):
             run(done, n - 3, 1)
             x_stage(4 * n + 9)
             run(sq, n + 1, 0)
+            if n == -1:
+                sq(0, 1)
+                sr(0)
             run(m2, n - 2, 1, 1)
             run(m2, n - 2, 1, 0)
             run(cr, n - 2, 1)
             run(hh, n, 0)
-            x_stage(4 * n + 10)
             run(hh, n, 1)
-            run(m1, n + 1, 1)
+            if n >= 0:
+                run(m1, n + 1, 1)
+            x_stage(4 * n + 10)
             if n == 0:
                 wb_rope()
             if n == 1:

@@ -133,8 +133,8 @@ def tile_multiheadlatentattention_pa_t_kernel(tc, x, Wqa, q_a_norm_w, Wqb, out):
 
         def wb_rope():
             nc.vector.tensor_copy(
-                out=wb_grp[:, 512:1024, :].rearrange("p (h f) t -> p h f t", h=HEADS),
-                in_=wb_raw[:].rearrange("p t (h z f) -> p z h f t", h=HEADS, z=2)[:, 1],
+                out=wb_grp[:, 512:1024, :].rearrange("p (h c i) t -> p h c t i", h=HEADS, i=4),
+                in_=wb_raw[:].rearrange("p t (h z c i) -> p z h c t i", h=HEADS, z=2, i=4)[:, 1],
             )
             nc.vector.quantize_mx(
                 out=wb_q[:, 512:1024].bitcast(FP8X4),
@@ -144,8 +144,8 @@ def tile_multiheadlatentattention_pa_t_kernel(tc, x, Wqa, q_a_norm_w, Wqb, out):
 
         def wb_nope():
             nc.vector.tensor_copy(
-                out=wb_grp[:, 0:512, :].rearrange("p (h f) t -> p h f t", h=HEADS),
-                in_=wb_raw[:].rearrange("p t (h z f) -> p z h f t", h=HEADS, z=2)[:, 0],
+                out=wb_grp[:, 0:512, :].rearrange("p (h c i) t -> p h c t i", h=HEADS, i=4),
+                in_=wb_raw[:].rearrange("p t (h z c i) -> p z h c t i", h=HEADS, z=2, i=4)[:, 0],
             )
             nc.vector.quantize_mx(
                 out=wb_q[:, 0:512].bitcast(FP8X4),
@@ -180,7 +180,10 @@ def tile_multiheadlatentattention_pa_t_kernel(tc, x, Wqa, q_a_norm_w, Wqb, out):
             at = (p - first) * 1024
             dst = st["gx", first][:, at : at + 1024].bitcast(F32).rearrange("p (a r u) -> p a r u", a=2, u=2)
             src = st["xt", p][:].rearrange("p a u r -> p a r u")
-            nc.scalar.copy(out=dst, in_=src)
+            if p in (5,):
+                nc.vector.tensor_copy(out=dst, in_=src)
+            else:
+                nc.scalar.copy(out=dst, in_=src)
 
         def qx(p):
             first, pairs = x_group(p)

import math
from contextlib import ExitStack

import concourse.bass as bass
import concourse.masks as masks
import concourse.mybir as mybir
import concourse.tile as tile

F32 = mybir.dt.float32
BF16 = mybir.dt.bfloat16
I32 = mybir.dt.int32
U32 = mybir.dt.uint32
U8 = mybir.dt.uint8
FP8X4 = mybir.dt.float8_e4m3fn_x4
ALU = mybir.AluOpType
ACT = mybir.ActivationFunctionType

P = 128
HEADS = 8
N_UNITS = 8
N_PAIRS = 16
EPS = 1e-6
SHARE = (0, 1)
FLOPS = 2 * 4096 * 512 * 512 + 2 * 4096 * 512 * 1024


def tile_multiheadlatentattention_pa_t_kernel(tc, x, Wqa, q_a_norm_w, Wqb, out):
    nc = tc.nc
    with ExitStack() as ctx:
        ctx.enter_context(tc.manual_schedule())
        const = ctx.enter_context(tc.tile_pool(name="const", bufs=1))
        psum = ctx.enter_context(tc.psum_pool(name="psum", bufs=1))
        work = ctx.enter_context(tc.tile_pool(name="work", bufs=3))
        outp = ctx.enter_context(tc.tile_pool(name="outp", bufs=3))

        x_units = x.flatten_outer_dims().rearrange("(u p i) d -> u p (i d)", u=N_UNITS, p=P, i=4)
        w_row = const.tile([P, 512], BF16, name="w_row")
        nc.gpsimd.memset(w_row[:], 0.0)
        nc.sync.dma_start(out=w_row[0:1, :], in_=q_a_norm_w.rearrange("(o r) -> o r", o=1))
        wa_raw = const.tile([P, 4, 512], BF16, name="wa_raw")
        nc.sync.dma_start(
            out=wa_raw[:].rearrange("p j c -> p (j c)"),
            in_=Wqa.rearrange("(p j) c -> p (j c)", p=P, j=4),
        )
        x_sb = []
        for u in range(N_UNITS):
            x_sb.append(const.tile([P, 2048], BF16, name="x_sb%d" % u))
        nc.sync.dma_start(out=x_sb[0][:, 0:1024], in_=x_units[0][:, 0:1024])
        nc.sync.dma_start(out=x_sb[0][:, 1024:2048], in_=x_units[0][:, 1024:2048])
        for u in range(1, 6):
            nc.sync.dma_start(out=x_sb[u][:], in_=x_units[u])
        wb_raw = const.tile([P, 4, 1024], BF16, name="wb_raw")
        nc.sync.dma_start(
            out=wb_raw[:].rearrange("p j n -> p (j n)"), in_=Wqb.rearrange("(p j) n -> p (j n)", p=P, j=4)
        )
        for u in range(6, N_UNITS):
            nc.sync.dma_start(out=x_sb[u][:], in_=x_units[u])

        pos = const.tile([P, 8], I32, name="pos")
        nc.gpsimd.iota(pos[:], pattern=[[512, 2], [1, 4]], base=0, channel_multiplier=4)
        ident_f = const.tile([P, P], F32, name="ident_f")
        masks.make_identity(nc, ident_f[:])
        eps_t = const.tile([P, 1], F32, name="eps_t")
        nc.vector.memset(eps_t[:], EPS)
        ones_b = const.tile([P, P], BF16, name="ones_b")
        nc.gpsimd.memset(ones_b[:], 1.0)
        w_bc = const.tile([P, 512], BF16, name="w_bc")

        def spread_gain():
            w_ps = psum.tile([P, 512], F32, name="w_ps", tag="ht")
            nc.tensor.matmul(out=w_ps[:], lhsT=ones_b[:], rhs=w_row[:], start=True, stop=True)
            nc.vector.tensor_copy(
                out=w_bc[:].rearrange("p (u m e) -> p u m e", u=2, e=2),
                in_=w_ps[:].rearrange("p (m u e) -> p u m e", u=2, e=2),
            )

        ratio = 10000.0 ** (-1.0 / 32.0)
        one = const.tile([P, 1], F32, name="one")
        nc.vector.memset(one[:], 1.0)
        turn = const.tile([P, 32], F32, name="turn")
        for f in range(4):
            nc.vector.tensor_scalar_mul(out=turn[:, f : f + 1], in0=one[:], scalar1=ratio**f / (2.0 * math.pi))
        for f in range(4, 32, 4):
            nc.vector.tensor_scalar_mul(out=turn[:, f : f + 4], in0=turn[:, 0:4], scalar1=ratio**f)
        turns = const.tile([P, 2, 8, 32], F32, name="turns")
        whole = const.tile([P, 2, 8, 32], I32, name="whole")
        frac = const.tile([P, 2, 8, 32], F32, name="frac")
        nc.vector.tensor_tensor(
            out=turns[:, 0],
            in0=pos[:].unsqueeze(2).to_broadcast([P, 8, 32]),
            in1=turn[:].unsqueeze(1).to_broadcast([P, 8, 32]),
            op=ALU.mult,
        )
        nc.vector.tensor_scalar_add(out=turns[:, 1], in0=turns[:, 0], scalar1=0.25)
        for s in range(2):
            nc.vector.tensor_copy(out=whole[:, s], in_=turns[:, s])
        for s in range(2):
            nc.vector.tensor_tensor(out=frac[:, s], in0=turns[:, s], in1=whole[:, s], op=ALU.subtract)
        sines = const.tile([P, 8, 32], F32, name="sines")
        warm = const.tile([P, 2], F32, name="warm")
        nc.scalar.activation(out=warm[:, 0:1], in_=one[:], func=ACT.Sin)
        tab = const.tile([P, 8, 2, 32], F32, name="tab")

        def tables():
            nc.scalar.activation(out=sines[:], in_=frac[:, 0], func=ACT.Sin, scale=2.0 * math.pi)
            nc.scalar.activation(out=tab[:, :, 0], in_=frac[:, 1], func=ACT.Sin, scale=2.0 * math.pi)
            nc.scalar.activation(out=warm[:, 1:2], in_=eps_t[:], func=ACT.Abs_reciprocal_sqrt)
            for e in range(2):
                nc.gpsimd.tensor_scalar(
                    out=tab[:, :, 1].rearrange("p c (j e) -> p c j e", e=2)[:, :, :, e],
                    in0=sines[:].rearrange("p c (j e) -> p c j e", e=2)[:, :, :, 1 - e],
                    scalar1=1.0 if e == 0 else -1.0,
                    scalar2=0.0,
                    op0=ALU.mult,
                    op1=ALU.add,
                )

        wa_grp = const.tile([P, 512, 4], BF16, name="wa_grp", align_bytes=64)
        for u in range(2):
            nc.vector.tensor_copy(
                out=wa_grp[:].rearrange("p (u m e) j -> p u m e j", u=2, e=2)[:, u],
                in_=wa_raw[:].rearrange("p j (m u e) -> p u m e j", u=2, e=2)[:, u],
            )
        wa_q = const.tile([P, 512], U32, name="wa_q", align_bytes=64)
        wa_s = const.tile([P, 512], U8, name="wa_s", align_bytes=64)
        nc.vector.quantize_mx(
            out=wa_q[:].bitcast(FP8X4), scales=wa_s[:], in_=wa_grp[:].rearrange("p c t -> p (c t)")
        )

        wb_grp = const.tile([P, 1024, 4], BF16, name="wb_grp", align_bytes=64)
        wb_q = const.tile([P, 1024], U32, name="wb_q", align_bytes=64)
        wb_s = const.tile([P, 1024], U8, name="wb_s", align_bytes=64)

        def wb_rope():
            nc.vector.tensor_copy(
                out=wb_grp[:, 512:1024, :].rearrange("p (h c i) t -> p h c t i", h=HEADS, i=4),
                in_=wb_raw[:].rearrange("p t (h z c i) -> p z h c t i", h=HEADS, z=2, i=4)[:, 1],
            )
            nc.vector.quantize_mx(
                out=wb_q[:, 512:1024].bitcast(FP8X4),
                scales=wb_s[:, 512:1024],
                in_=wb_grp[:, 512:1024, :].rearrange("p c t -> p (c t)"),
            )

        def wb_nope():
            nc.vector.tensor_copy(
                out=wb_grp[:, 0:512, :].rearrange("p (h c i) t -> p h c t i", h=HEADS, i=4),
                in_=wb_raw[:].rearrange("p t (h z c i) -> p z h c t i", h=HEADS, z=2, i=4)[:, 0],
            )
            nc.vector.quantize_mx(
                out=wb_q[:, 0:512].bitcast(FP8X4),
                scales=wb_s[:, 0:512],
                in_=wb_grp[:, 0:512, :].rearrange("p c t -> p (c t)"),
            )

        x_q = const.tile([P, N_PAIRS * 256], U32, name="x_q", align_bytes=64)
        x_s = const.tile([P, N_PAIRS * 256], U8, name="x_s", align_bytes=64)

        st = {}

        def tx(p):
            xt = psum.tile([P, 2, 2, P], F32, name="xt", tag=("r0", "n0", "r1", "n1")[p % 4])
            st["xt", p] = xt
            for a in range(2):
                k = 2 * p + a
                words = x_sb[k // 4][:].bitcast(F32)
                for u in range(2):
                    lo = (k % 4) * 256
                    nc.tensor.transpose(xt[:, a, u, :], words[:, lo + u : lo + 256 : 2], ident_f[:])

        def x_group(p):
            return (p, 1) if p < 2 else (p // 2 * 2, 2)

        def cx(p):
            first, pairs = x_group(p)
            if p == first:
                st["gx", first] = work.tile(
                    [P, 1024 * pairs], BF16, name="gx", tag="gx%d" % pairs, bufs=4, align_bytes=64
                )
            at = (p - first) * 1024
            dst = st["gx", first][:, at : at + 1024].bitcast(F32).rearrange("p (a r u) -> p a r u", a=2, u=2)
            src = st["xt", p][:].rearrange("p a u r -> p a r u")
            if p in (5,):
                nc.vector.tensor_copy(out=dst, in_=src)
            else:
                nc.scalar.copy(out=dst, in_=src)

        def qx(p):
            first, pairs = x_group(p)
            if p == first + pairs - 1:
                cols = slice(first * 256, (p + 1) * 256)
                nc.vector.quantize_mx(out=x_q[:, cols].bitcast(FP8X4), scales=x_s[:, cols], in_=st["gx", first][:])

        def m1(p, a):
            k = 2 * p + a
            c = psum.tile([P, 512], F32, name="c", tag="c%d" % (k % 3))
            st["c", p, a] = c
            nc.tensor.matmul_mx(
                out=c[:],
                lhsT=x_q[:, k * P : (k + 1) * P].bitcast(FP8X4),
                lhsT_scale=x_s[:, k * P : (k + 1) * P],
                rhs=wa_q[:].bitcast(FP8X4),
                rhs_scale=wa_s[:],
                start=True,
                stop=True,
            )

        def sq(p, a):
            if a == 0:
                st["ssq", p] = work.tile([P, 2], F32, name="ssq", tag="ssq")
            junk = work.tile([P, 512], BF16, name="junk", tag="junk")
            nc.scalar.activation(out=junk[:], in_=st["c", p, a][:], func=ACT.Square, accum_out=st["ssq", p][:, a : a + 1])

        def sr(p):
            rstd = work.tile([P, 2], F32, name="rstd", tag="rstd")
            st["rstd", p] = rstd
            nc.scalar.activation(
                out=rstd[:],
                in_=st["ssq", p][:],
                func=ACT.Abs_reciprocal_sqrt,
                scale=1.0 / 512.0,
                bias=eps_t[:],
            )

        def hh(p, a):
            h = work.tile([P, 512], BF16, name="h%d" % a, tag="h%d" % a)
            st["h", p, a] = h
            nc.vector.scalar_tensor_tensor(
                out=h[:],
                in0=st["c", p, a][:],
                scalar=st["rstd", p][:, a : a + 1],
                in1=w_bc[:],
                op0=ALU.mult,
                op1=ALU.mult,
            )

        def th(p):
            ht = psum.tile([P, 2, 2, P], F32, name="ht", tag="ht")
            st["ht", p] = ht
            for a in range(2):
                words = st["h", p, a][:].bitcast(F32)
                for u in range(2):
                    nc.tensor.transpose(ht[:, a, u, :], words[:, u * P : (u + 1) * P], ident_f[:])

        def ch(p):
            gh = work.tile([P, 1024], BF16, name="gh", tag="gh", align_bytes=64)
            st["gh", p] = gh
            nc.scalar.copy(
                out=gh[:].bitcast(F32).rearrange("p (a r u) -> p a r u", a=2, u=2),
                in_=st["ht", p][:].rearrange("p a u r -> p a r u"),
            )

        def qh(p):
            hq = work.tile([P, 256], U32, name="hq", tag="hq", align_bytes=64)
            hs = work.tile([P, 256], U8, name="hs", tag="hs", align_bytes=64)
            st["hq", p] = (hq, hs)
            nc.vector.quantize_mx(out=hq[:].bitcast(FP8X4), scales=hs[:], in_=st["gh", p][:])

        def m2(p, a, z):
            kind = "nr"[z]
            acc = psum.tile([P, 512], F32, name="%s%d" % (kind, a), tag="%s%d" % (kind, a))
            st[kind, p, a] = acc
            hq, hs = st["hq", p]
            nc.tensor.matmul_mx(
                out=acc[:],
                lhsT=hq[:, a * P : (a + 1) * P].bitcast(FP8X4),
                lhsT_scale=hs[:, a * P : (a + 1) * P],
                rhs=wb_q[:, z * 512 : (z + 1) * 512].bitcast(FP8X4),
                rhs_scale=wb_s[:, z * 512 : (z + 1) * 512],
                start=True,
                stop=True,
            )

        def out_part(k):
            u, i = divmod(k, 4)
            if u < N_UNITS - 3:
                first, width = 0, 4
            elif u < N_UNITS - 1 or i < 2:
                first, width = i // 2 * 2, 2
            else:
                first, width = i, 1
            if ("o", u, first) not in st:
                st["o", u, first] = outp.tile(
                    [P, HEADS, width, P], F32, name="o_sb", tag="o_sb%d" % width, bufs=2 if width == 1 else 3
                )
            return st["o", u, first][:, :, i - first, :]

        def cn(p, a):
            k = 2 * p + a
            nc.scalar.copy(
                out=out_part(k)[:, :, 0:64],
                in_=st["n", p, a][:].rearrange("p (h f) -> p h f", h=HEADS),
            )

        def prod_tile(p, a):
            if ("t", p, a) not in st:
                st["t", p, a] = work.tile([P, 2, 512], F32, name="prod", tag="prod")
            return st["t", p, a]

        def products(engine, p, a, r, lo, hi):
            shape = [P, 2, 2 * (hi - lo), 32]
            engine.tensor_tensor(
                out=prod_tile(p, a)[:, :, lo * 64 : hi * 64].rearrange("p z (g f) -> p z g f", f=32),
                in0=r.rearrange("p (g f) -> p g f", f=32).unsqueeze(1).to_broadcast(shape),
                in1=tab[:, (2 * p + a) % 8].unsqueeze(2).to_broadcast(shape),
                op=ALU.mult,
            )

        def shared(p, a):
            return SHARE[a] if p < N_PAIRS - 3 else 0

        def tt(p, a):
            hi = HEADS - shared(p, a)
            products(nc.vector, p, a, st["r", p, a][:, 0 : hi * 64], 0, hi)

        def cr(p, a):
            s = shared(p, a)
            if s:
                r_sb = work.tile([P, s * 64], F32, name="r_sb", tag="r_sb%d" % a)
                st["r_sb", p, a] = r_sb
                nc.scalar.copy(out=r_sb[:], in_=st["r", p, a][:, 512 - s * 64 : 512])

        def pr(p, a):
            s = shared(p, a)
            if s:
                products(nc.gpsimd, p, a, st["r_sb", p, a][:], HEADS - s, HEADS)

        def ad(p, a):
            k = 2 * p + a
            prod = st["t", p, a]
            engine = nc.vector if p == N_PAIRS - 1 else nc.gpsimd
            engine.tensor_tensor(
                out=out_part(k)[:, :, 64:128].rearrange("p h (i e) -> p h i e", e=2),
                in0=prod[:, 0].rearrange("p (h i e) -> p h i e", h=HEADS, e=2),
                in1=prod[:, 1].rearrange("p (h i e) -> p h i e", h=HEADS, e=2)[:, :, :, ::-1],
                op=ALU.add,
            )

        def store(u, lo, hi):
            dst = out[u // 2].rearrange("h (q p i) f -> q p h (i f)", q=2, p=P, i=4)[u % 2]
            nc.sync.dma_start(
                out=dst[:, :, lo * P : hi * P],
                in_=st["o", u, lo][:].rearrange("p h i f -> p h (i f)"),
            )

        def done(p, a):
            if p == N_PAIRS - 1:
                store(N_UNITS - 1, 2 + a, 3 + a)
            elif p >= N_PAIRS - 6 and a == 1:
                store(p // 2, p % 2 * 2, p % 2 * 2 + 2)
            elif p % 2 == 1 and a == 1:
                store(p // 2, 0, 4)

        def run(stage, p, *rest):
            if 0 <= p < N_PAIRS:
                stage(p, *rest)

        def x_stage(q):
            run(tx, q)
            run(cx, q - 2)
            run(qx, q - 3)

        tables()
        spread_gain()
        for n in range(-2, N_PAIRS + 4):
            run(tt, n - 3, 0)
            run(th, n - 1)
            x_stage(4 * n + 7)
            if n > 0:
                run(sq, n, 1)
            run(ch, n - 1)
            if n > 0:
                run(sr, n)
            run(m1, n + 1, 0)
            if n == -1:
                m1(0, 1)
            x_stage(4 * n + 8)
            run(cn, n - 3, 0)
            run(pr, n - 3, 1)
            run(qh, n - 2)
            run(ad, n - 3, 0)
            run(done, n - 3, 0)
            run(m2, n - 2, 0, 1)
            run(m2, n - 2, 0, 0)
            run(cn, n - 3, 1)
            run(tt, n - 3, 1)
            run(ad, n - 3, 1)
            run(done, n - 3, 1)
            x_stage(4 * n + 9)
            run(sq, n + 1, 0)
            if n == -1:
                sq(0, 1)
                sr(0)
            run(m2, n - 2, 1, 1)
            run(m2, n - 2, 1, 0)
            run(cr, n - 2, 1)
            run(hh, n, 0)
            run(hh, n, 1)
            if n >= 0:
                run(m1, n + 1, 1)
            x_stage(4 * n + 10)
            if n == 0:
                wb_rope()
            if n == 1:
                wb_nope()
